import numpy as np
import ml_dtypes


def mxq(x, axis, fmt="e4m3"):
    dtype, down = {"e4m3": (ml_dtypes.float8_e4m3fn, 7), "e5m2": (ml_dtypes.float8_e5m2, 14)}[fmt]
    v = np.moveaxis(np.asarray(x, np.float32).astype(ml_dtypes.bfloat16).astype(np.float64), axis, -1)
    blocks = v.reshape(v.shape[:-1] + (-1, 32))
    amax = np.abs(blocks).max(-1, keepdims=True)
    byte = np.maximum(np.where(amax > 0, np.frexp(amax)[1] - 1 + 127, 0) - down, 1)
    scale = np.exp2(byte - 127.0)
    codes = (blocks / scale).astype(np.float32).astype(dtype).astype(np.float64)
    return np.moveaxis((codes * scale).reshape(v.shape), -1, axis)


WIDE = False


def mx_kscale(k):
    if not WIDE:
        return np.ones(k)
    levels = np.array([10, -10, 5, -5, 0])
    if k % 512:
        return np.exp2(np.random.permutation(np.resize(levels, k // 32))).repeat(32)
    a = np.empty((k // 512, 16))
    for p in range(k // 512):
        a[p, :8] = np.random.permutation(np.resize(levels, 8))
        for g in range(8):
            far = levels[np.abs(levels - a[p, g]) >= 10]
            a[p, g + 8] = far[np.random.randint(len(far))]
    return np.exp2(a.ravel()).repeat(32)


BF16 = ml_dtypes.bfloat16


def bf(x):
    return np.asarray(x, np.float32).astype(BF16)


def f64(x):
    return np.asarray(x).astype(np.float64)


N, G, GIN, GOUT = 1024, 8, 512, 512

P0 = np.array([0.5, 1.0, 0.5, 0.3])
Q0 = np.array([0.5, 0.3, 0.2])


def rational(y, p, q):
    p = p[None, :, :, None]
    q = q[None, :, :, None]
    y2 = y * y
    y3 = y2 * y
    num = p[:, :, 0] + p[:, :, 1] * y + p[:, :, 2] * y2 + p[:, :, 3] * y3
    den = 1.0 + np.abs(q[:, :, 0] * y + q[:, :, 1] * y2 + q[:, :, 2] * y3)
    return num / den


def draw0():
    s = mx_kscale(GIN)
    return {"x": bf(np.random.standard_normal((N, G * GIN)) * np.tile(s, G)),
            "W": bf(np.random.standard_normal((G, GIN, GOUT)) / np.sqrt(GIN) / s[None, :, None]),
            "b": bf(np.random.standard_normal((G, GOUT)) * 0.3),
            "p": bf(P0 + 0.1 * np.random.standard_normal((G, P0.size))),
            "q": bf(Q0 + 0.05 * np.random.standard_normal((G, Q0.size)))}


def core(x, W, b, p, q):
    n = x.shape[0]
    xg = f64(x).reshape(n, G, GIN)
    xq = mxq(xg, 2, "e4m3")
    wq = mxq(f64(W), 1, "e4m3")
    y = (xq.transpose(1, 0, 2) @ wq).transpose(1, 0, 2) + f64(b)[None]
    out = rational(y, f64(p), f64(q))
    return out.reshape(n, G * GOUT)


def e4m3fn_bytes(y):
    return np.clip(np.asarray(y, np.float64), -448.0, 448.0).astype(np.float32).astype(ml_dtypes.float8_e4m3fn).view(np.uint8)


def e4m3fn_values(b):
    return np.asarray(b, np.uint8).view(ml_dtypes.float8_e4m3fn).astype(np.float64)


def setup_inputs():
    d = draw0()
    x0 = np.asarray(d['x']).astype(np.float64)
    s = (np.max(np.abs(x0), axis=(0,), keepdims=True) / 448.0).astype(np.float32)
    out = {}
    for k, v in d.items():
        if k == 'x':
            out['x_bytes'] = e4m3fn_bytes(x0 / s.astype(np.float64))
            out['x_scale'] = s
        else:
            out[k] = v
    return out


def reference(x_bytes, x_scale, W, b, p, q):
    return core(e4m3fn_values(x_bytes) * x_scale.astype(np.float64), W, b, p, q)

@@ -1,0 +1,264 @@
+from contextlib import ExitStack
+
+import concourse.mybir as mybir
+from concourse.masks import make_identity
+
+ROWS, GROUPS, K_IN, K_OUT = 1024, 8, 512, 512
+FLOPS = 2 * ROWS * GROUPS * K_IN * K_OUT
+
+F32 = mybir.dt.float32
+BF16 = mybir.dt.bfloat16
+U32 = mybir.dt.uint32
+U8 = mybir.dt.uint8
+FP8 = mybir.dt.float8_e4m3fn
+FP8X4 = mybir.dt.float8_e4m3fn_x4
+ACT = mybir.ActivationFunctionType
+ALU = mybir.AluOpType
+
+P = 128
+ROW_TILES = ROWS // P
+N_TILE = 512
+HALVES = ROWS // N_TILE
+O_TILES = K_OUT // P
+
+
+def tile_groupkanlayer_kernel(tc, x_bytes, x_scale, W, b, p, q, out):
+    nc = tc.nc
+    with ExitStack() as ctx:
+        ctx.enter_context(tc.manual_schedule())
+        const = ctx.enter_context(tc.tile_pool(name="const", bufs=1))
+        wstage = ctx.enter_context(tc.tile_pool(name="wstage", bufs=2))
+        xstage = ctx.enter_context(tc.tile_pool(name="xstage", bufs=4))
+        gstage = ctx.enter_context(tc.tile_pool(name="gstage", bufs=2))
+        work = ctx.enter_context(tc.tile_pool(name="work", bufs=8))
+        ps_x = ctx.enter_context(tc.psum_pool(name="ps_x", bufs=2))
+        ps_a = ctx.enter_context(tc.psum_pool(name="ps_a", bufs=2))
+        ps_y = ctx.enter_context(tc.psum_pool(name="ps_y", bufs=4))
+
+        ones = const.tile([P, 1], F32, name="ones")
+        nc.vector.memset(ones[:], 1.0)
+        junk = const.tile([P, 1], F32, name="junk")
+        nc.scalar.activation(out=junk[:], in_=ones[:], func=ACT.Abs_reciprocal_sqrt)
+
+        ident = const.tile([P, P], F32, name="ident")
+        make_identity(nc, ident[:])
+
+        p_bf = const.tile([P, GROUPS * 4], BF16, name="p_bf")
+        q_bf = const.tile([P, GROUPS * 3], BF16, name="q_bf")
+        b_rows = const.tile([P, P], BF16, name="b_rows")
+        nc.vector.memset(b_rows[:].bitcast(F32), 0.0)
+
+        xb, sc, w_raw = [], [], []
+        scale_row = x_scale.rearrange("o k -> (o k)")
+        for g in range(GROUPS):
+            cols = slice(g * K_IN, (g + 1) * K_IN)
+            sc_g = const.tile([P, K_IN], F32, name="sc%d" % g)
+            nc.sync.dma_start(out=sc_g[:], in_=scale_row[cols].partition_broadcast(P))
+            xb_g = const.tile([P, ROW_TILES, K_IN], U8, name="xbytes%d" % g)
+            x_view = x_bytes[:, cols].rearrange("(r p) c -> p r c", p=P)
+            if g == 0:
+                nc.sync.dma_start(out=xb_g[:, 0:4, :], in_=x_view[:, 0:4, :])
+            w_g = const.tile([P, 4, K_OUT], BF16, name="wraw%d" % g)
+            nc.sync.dma_start(out=w_g[:], in_=W[g].rearrange("(p j) o -> p j o", j=4))
+            if g == 0:
+                nc.sync.dma_start(out=xb_g[:, 4:8, :], in_=x_view[:, 4:8, :])
+                nc.sync.dma_start(out=b_rows[0 : GROUPS * O_TILES, :], in_=b.rearrange("g (c o) -> (g c) o", o=P))
+                nc.sync.dma_start(out=p_bf[:], in_=p.rearrange("g c -> (g c)").partition_broadcast(P))
+                nc.sync.dma_start(out=q_bf[:], in_=q.rearrange("g c -> (g c)").partition_broadcast(P))
+            else:
+                nc.sync.dma_start(out=xb_g[:], in_=x_view)
+            sc.append(sc_g)
+            xb.append(xb_g)
+            w_raw.append(w_g)
+
+        p_f = const.tile([P, GROUPS * 4], F32, name="p_f")
+        q_f = const.tile([P, GROUPS * 3], F32, name="q_f")
+        b_f = const.tile([P, P], F32, name="b_f")
+        bT = const.tile([P, GROUPS * O_TILES], F32, name="bT")
+
+        def prepare_parameters():
+            nc.vector.tensor_copy(out=b_f[:], in_=b_rows[:])
+            b_ps = ps_x.tile([P, P], F32, name="xt")
+            nc.tensor.transpose(b_ps[:], b_f[:], ident[:])
+            nc.vector.tensor_copy(out=p_f[:], in_=p_bf[:])
+            nc.vector.tensor_copy(out=q_f[:], in_=q_bf[:])
+            nc.vector.tensor_copy(out=bT[:], in_=b_ps[:, 0 : GROUPS * O_TILES])
+
+        xc = [const.tile([P, ROWS], U32, name="xc%d" % g, align_bytes=64) for g in range(GROUPS)]
+        xsc = [const.tile([P, ROWS], U8, name="xsc%d" % g, align_bytes=64) for g in range(GROUPS)]
+        wc = [const.tile([P, K_OUT], U32, name="wc%d" % g, align_bytes=64) for g in range(GROUPS)]
+        wsc = [const.tile([P, K_OUT], U8, name="wsc%d" % g, align_bytes=64) for g in range(GROUPS)]
+
+        state = {}
+
+        def w_interleave(g, piece):
+            if piece == 0:
+                state["w_grp"] = wstage.tile([P, K_OUT, 4], BF16, name="w_grp", align_bytes=64)
+            och = slice(piece * P, (piece + 1) * P)
+            nc.scalar.copy(out=state["w_grp"][:, och, :], in_=w_raw[g][:, :, och].rearrange("p j o -> p o j"))
+
+        def w_quantize(g):
+            nc.vector.quantize_mx(
+                out=wc[g][:].bitcast(FP8X4), scales=wsc[g][:],
+                in_=state["w_grp"][:].rearrange("p o j -> p (o j)"),
+            )
+
+        def x_widen(j):
+            c, i = divmod(j, 4)
+            g, nb = divmod(c, HALVES)
+            rt = nb * 4 + i
+            if i == 0:
+                state["grp"] = gstage.tile([P, 4 * N_TILE], BF16, name="grp", align_bytes=64)
+            if i % 2 == 0:
+                state["xt"] = ps_x.tile([P, 2, 2, P], F32, name="xt")
+            xs = xstage.tile([P, K_IN], BF16, name="xs")
+            nc.vector.tensor_tensor(out=xs[:], in0=xb[g][:, rt, :].bitcast(FP8), in1=sc[g][:], op=ALU.mult)
+            words = xs[:].bitcast(F32)
+            for u in range(2):
+                nc.tensor.transpose(state["xt"][:, i % 2, u, :], words[:, u : K_IN // 2 : 2], ident[:])
+
+        def x_exit(j):
+            pair = (j % 4) // 2
+            nc.scalar.copy(
+                out=state["grp"][:].bitcast(F32)[:, pair * 512 : (pair + 1) * 512].rearrange(
+                    "p (a r u) -> p a r u", a=2, u=2
+                ),
+                in_=state["xt"][:].rearrange("p a u r -> p a r u"),
+            )
+            if j % 4 == 3:
+                state["grp_done"] = state["grp"]
+
+        def x_quantize(c):
+            g, nb = divmod(c, HALVES)
+            tok = slice(nb * N_TILE, (nb + 1) * N_TILE)
+            nc.vector.quantize_mx(out=xc[g][:, tok].bitcast(FP8X4), scales=xsc[g][:, tok], in_=state["grp_done"][:])
+
+        TILES = GROUPS * HALVES * O_TILES
+        acc_of, yt_of, y_of, num_of, den_of, rec_of = {}, {}, {}, {}, {}, {}
+
+        def where(t):
+            c, oc = divmod(t, O_TILES)
+            g, nb = divmod(c, HALVES)
+            return g, nb, oc
+
+        def pcoef(t, i):
+            g = where(t)[0]
+            return p_f[:, 4 * g + i : 4 * g + i + 1]
+
+        def qcoef(t, i):
+            g = where(t)[0]
+            return q_f[:, 3 * g + i : 3 * g + i + 1]
+
+        def mm(t):
+            g, nb, oc = where(t)
+            tok = slice(nb * N_TILE, (nb + 1) * N_TILE)
+            och = slice(oc * P, (oc + 1) * P)
+            acc = ps_a.tile([P, N_TILE], F32, name="acc")
+            nc.tensor.matmul_mx(
+                out=acc[:], lhsT=wc[g][:, och].bitcast(FP8X4), lhsT_scale=wsc[g][:, och],
+                rhs=xc[g][:, tok].bitcast(FP8X4), rhs_scale=xsc[g][:, tok], start=True, stop=True,
+            )
+            acc_of[t] = acc
+
+        def add_bias(t):
+            g, nb, oc = where(t)
+            col = g * O_TILES + oc
+            yT = work.tile([P, N_TILE], F32, name="yT", bufs=3)
+            nc.scalar.activation(out=yT[:], in_=acc_of[t][:], func=ACT.Identity, bias=bT[:, col : col + 1], scale=1.0)
+            yt_of[t] = yT
+
+        def flip(t):
+            y = ps_y.tile([P, N_TILE], F32, name="y")
+            for j in range(4):
+                blk = slice(j * P, (j + 1) * P)
+                nc.tensor.transpose(y[:, blk], yt_of[t][:, blk], ident[:])
+            y_of[t] = y
+
+        def den_first(t):
+            den = work.tile([P, N_TILE], F32, name="den")
+            nc.scalar.activation(out=den[:], in_=y_of[t][:], func=ACT.Identity, bias=qcoef(t, 1), scale=qcoef(t, 2))
+            den_of[t] = den
+
+        def num_first(t):
+            num = work.tile([P, N_TILE], F32, name="num")
+            nc.scalar.activation(out=num[:], in_=y_of[t][:], func=ACT.Identity, bias=pcoef(t, 2), scale=pcoef(t, 3))
+            num_of[t] = num
+
+        def times_y(tile_of, t):
+            nc.vector.tensor_tensor(out=tile_of[t][:], in0=y_of[t][:], in1=tile_of[t][:], op=ALU.mult)
+
+        def plus_times_y(tile_of, t, coef):
+            nc.vector.scalar_tensor_tensor(
+                out=tile_of[t][:], in0=tile_of[t][:], scalar=coef, in1=y_of[t][:], op0=ALU.add, op1=ALU.mult
+            )
+
+        def den_abs(t):
+            nc.scalar.activation(out=den_of[t][:], in_=den_of[t][:], func=ACT.Abs)
+
+        def den_rsqrt(t):
+            nc.scalar.activation(out=den_of[t][:], in_=den_of[t][:], func=ACT.Abs_reciprocal_sqrt, bias=ones[:], scale=1.0)
+
+        def den_square(t):
+            rec = work.tile([P, N_TILE], F32, name="rec", bufs=2)
+            nc.gpsimd.tensor_tensor(out=rec[:], in0=den_of[t][:], in1=den_of[t][:], op=ALU.mult)
+            rec_of[t] = rec
+
+        def finish(t):
+            g, nb, oc = where(t)
+            tok = slice(nb * N_TILE, (nb + 1) * N_TILE)
+            nc.vector.scalar_tensor_tensor(
+                out=num_of[t][:], in0=num_of[t][:], scalar=pcoef(t, 0), in1=rec_of[t][:], op0=ALU.add, op1=ALU.mult
+            )
+            nc.sync.dma_start(
+                out=out[tok, g * K_OUT + oc * P : g * K_OUT + (oc + 1) * P].rearrange("(j n) o -> n j o", n=P),
+                in_=num_of[t][:].rearrange("n (j o) -> n j o", j=4),
+            )
+
+        def live(t):
+            return 0 <= t < TILES
+
+        for j in range(4):
+            x_widen(j)
+            w_interleave(0, j)
+            if j % 2 == 1:
+                x_exit(j)
+        w_quantize(0)
+        x_quantize(0)
+        prepare_parameters()
+
+        X_LEAD = 7
+        for s in range(-3, TILES + 4):
+            j = s + X_LEAD
+            if live(s):
+                den_first(s)
+            if 4 <= j < TILES:
+                x_widen(j)
+            if live(s + 1):
+                add_bias(s + 1)
+                flip(s + 1)
+            if (s + 3) % 4 == 0 and 1 <= (s + 3) // 4 < GROUPS * HALVES:
+                x_quantize((s + 3) // 4)
+            if (s + 4) % 8 == 0 and 1 <= (s + 4) // 8 < GROUPS:
+                w_quantize((s + 4) // 8)
+            if live(s - 4):
+                finish(s - 4)
+            if live(s - 2):
+                den_square(s - 2)
+            if live(s):
+                num_first(s)
+            if live(s - 1):
+                times_y(num_of, s - 1)
+                den_abs(s - 1)
+            if live(s):
+                times_y(den_of, s)
+            if live(s + 2):
+                mm(s + 2)
+            if 4 <= j < TILES and j % 2 == 1:
+                x_exit(j)
+            if s % 2 == 1 and 1 <= (s + 11) // 8 < GROUPS:
+                w_interleave((s + 11) // 8, ((s + 11) % 8) // 2)
+            if live(s - 1):
+                plus_times_y(num_of, s - 1, pcoef(s - 1, 1))
+                den_rsqrt(s - 1)
+            if live(s):
+                plus_times_y(den_of, s, qcoef(s, 0))

@@ -30,10 +30,11 @@ def tile_groupkanlayer_kernel(tc, x_bytes, x_scale, W, b, p, q, out):
         wstage = ctx.enter_context(tc.tile_pool(name="wstage", bufs=2))
         xstage = ctx.enter_context(tc.tile_pool(name="xstage", bufs=4))
         gstage = ctx.enter_context(tc.tile_pool(name="gstage", bufs=2))
-        work = ctx.enter_context(tc.tile_pool(name="work", bufs=8))
+        work = ctx.enter_context(tc.tile_pool(name="work", bufs=4))
         ps_x = ctx.enter_context(tc.psum_pool(name="ps_x", bufs=2))
         ps_a = ctx.enter_context(tc.psum_pool(name="ps_a", bufs=2))
-        ps_y = ctx.enter_context(tc.psum_pool(name="ps_y", bufs=4))
+        ps_u = ctx.enter_context(tc.psum_pool(name="ps_u", bufs=2))
+        ps_n = ctx.enter_context(tc.psum_pool(name="ps_n", bufs=2))
 
         ones = const.tile([P, 1], F32, name="ones")
         nc.vector.memset(ones[:], 1.0)
@@ -90,6 +91,7 @@ def tile_groupkanlayer_kernel(tc, x_bytes, x_scale, W, b, p, q, out):
         wsc = [const.tile([P, K_OUT], U8, name="wsc%d" % g, align_bytes=64) for g in range(GROUPS)]
 
         state = {}
+        grp_of = {}
 
         def w_interleave(g, piece):
             if piece == 0:
@@ -108,33 +110,36 @@ def tile_groupkanlayer_kernel(tc, x_bytes, x_scale, W, b, p, q, out):
             g, nb = divmod(c, HALVES)
             rt = nb * 4 + i
             if i == 0:
-                state["grp"] = gstage.tile([P, 4 * N_TILE], BF16, name="grp", align_bytes=64)
+                grp_of[c] = gstage.tile([P, 4 * N_TILE], BF16, name="grp", align_bytes=64)
             if i % 2 == 0:
                 state["xt"] = ps_x.tile([P, 2, 2, P], F32, name="xt")
             xs = xstage.tile([P, K_IN], BF16, name="xs")
             nc.vector.tensor_tensor(out=xs[:], in0=xb[g][:, rt, :].bitcast(FP8), in1=sc[g][:], op=ALU.mult)
-            words = xs[:].bitcast(F32)
+            state["xs"] = xs
+
+        def x_turn(j):
+            words = state["xs"][:].bitcast(F32)
             for u in range(2):
-                nc.tensor.transpose(state["xt"][:, i % 2, u, :], words[:, u : K_IN // 2 : 2], ident[:])
+                nc.tensor.transpose(state["xt"][:, j % 2, u, :], words[:, u : K_IN // 2 : 2], ident[:])
+            if j % 2 == 1:
+                state["xt_done"] = state["xt"]
 
         def x_exit(j):
             pair = (j % 4) // 2
             nc.scalar.copy(
-                out=state["grp"][:].bitcast(F32)[:, pair * 512 : (pair + 1) * 512].rearrange(
+                out=grp_of[j // 4][:].bitcast(F32)[:, pair * 512 : (pair + 1) * 512].rearrange(
                     "p (a r u) -> p a r u", a=2, u=2
                 ),
-                in_=state["xt"][:].rearrange("p a u r -> p a r u"),
+                in_=state["xt_done"][:].rearrange("p a u r -> p a r u"),
             )
-            if j % 4 == 3:
-                state["grp_done"] = state["grp"]
 
         def x_quantize(c):
             g, nb = divmod(c, HALVES)
             tok = slice(nb * N_TILE, (nb + 1) * N_TILE)
-            nc.vector.quantize_mx(out=xc[g][:, tok].bitcast(FP8X4), scales=xsc[g][:, tok], in_=state["grp_done"][:])
+            nc.vector.quantize_mx(out=xc[g][:, tok].bitcast(FP8X4), scales=xsc[g][:, tok], in_=grp_of[c][:])
 
         TILES = GROUPS * HALVES * O_TILES
-        acc_of, yt_of, y_of, num_of, den_of, rec_of = {}, {}, {}, {}, {}, {}
+        acc_of, s_of, c_of, a_of, d_of, u_of, n_of, den_of = {}, {}, {}, {}, {}, {}, {}, {}
 
         def where(t):
             c, oc = divmod(t, O_TILES)
@@ -149,69 +154,76 @@ def tile_groupkanlayer_kernel(tc, x_bytes, x_scale, W, b, p, q, out):
             g = where(t)[0]
             return q_f[:, 3 * g + i : 3 * g + i + 1]
 
-        def mm(t):
+        def bias(t):
+            g, nb, oc = where(t)
+            col = g * O_TILES + oc
+            return bT[:, col : col + 1]
+
+        def mm(t, first):
             g, nb, oc = where(t)
             tok = slice(nb * N_TILE, (nb + 1) * N_TILE)
             och = slice(oc * P, (oc + 1) * P)
-            acc = ps_a.tile([P, N_TILE], F32, name="acc")
+            if first:
+                acc_of[t] = ps_a.tile([P, N_TILE], F32, name="acc")
             nc.tensor.matmul_mx(
-                out=acc[:], lhsT=wc[g][:, och].bitcast(FP8X4), lhsT_scale=wsc[g][:, och],
+                out=acc_of[t][:], lhsT=wc[g][:, och].bitcast(FP8X4), lhsT_scale=wsc[g][:, och],
                 rhs=xc[g][:, tok].bitcast(FP8X4), rhs_scale=xsc[g][:, tok], start=True, stop=True,
             )
-            acc_of[t] = acc
 
-        def add_bias(t):
-            g, nb, oc = where(t)
-            col = g * O_TILES + oc
-            yT = work.tile([P, N_TILE], F32, name="yT", bufs=3)
-            nc.scalar.activation(out=yT[:], in_=acc_of[t][:], func=ACT.Identity, bias=bT[:, col : col + 1], scale=1.0)
-            yt_of[t] = yT
+        def square_y(t):
+            s = work.tile([P, N_TILE], F32, name="s", bufs=7)
+            nc.scalar.activation(out=s[:], in_=acc_of[t][:], func=ACT.Square, bias=bias(t), scale=1.0)
+            s_of[t] = s
 
-        def flip(t):
-            y = ps_y.tile([P, N_TILE], F32, name="y")
-            for j in range(4):
-                blk = slice(j * P, (j + 1) * P)
-                nc.tensor.transpose(y[:, blk], yt_of[t][:, blk], ident[:])
-            y_of[t] = y
+        def aff_c(t):
+            c = work.tile([P, N_TILE], F32, name="c", bufs=3)
+            nc.vector.tensor_scalar(out=c[:], in0=s_of[t][:], scalar1=qcoef(t, 2), scalar2=qcoef(t, 0), op0=ALU.mult, op1=ALU.add)
+            c_of[t] = c
 
-        def den_first(t):
-            den = work.tile([P, N_TILE], F32, name="den")
-            nc.scalar.activation(out=den[:], in_=y_of[t][:], func=ACT.Identity, bias=qcoef(t, 1), scale=qcoef(t, 2))
-            den_of[t] = den
+        def aff_a(t):
+            a = work.tile([P, N_TILE], F32, name="a", bufs=5)
+            nc.vector.tensor_scalar(out=a[:], in0=s_of[t][:], scalar1=pcoef(t, 3), scalar2=pcoef(t, 1), op0=ALU.mult, op1=ALU.add)
+            a_of[t] = a
 
-        def num_first(t):
-            num = work.tile([P, N_TILE], F32, name="num")
-            nc.scalar.activation(out=num[:], in_=y_of[t][:], func=ACT.Identity, bias=pcoef(t, 2), scale=pcoef(t, 3))
-            num_of[t] = num
+        def aff_d(t):
+            d = work.tile([P, N_TILE], F32, name="d", bufs=4)
+            nc.gpsimd.tensor_scalar(out=d[:], in0=s_of[t][:], scalar1=qcoef(t, 1), scalar2=0.0, op0=ALU.mult, op1=ALU.add)
+            d_of[t] = d
+
+        def aff_b(t):
+            nc.gpsimd.tensor_scalar(out=s_of[t][:], in0=s_of[t][:], scalar1=pcoef(t, 2), scalar2=pcoef(t, 0), op0=ALU.mult, op1=ALU.add)
 
         def times_y(tile_of, t):
-            nc.vector.tensor_tensor(out=tile_of[t][:], in0=y_of[t][:], in1=tile_of[t][:], op=ALU.mult)
-
-        def plus_times_y(tile_of, t, coef):
             nc.vector.scalar_tensor_tensor(
-                out=tile_of[t][:], in0=tile_of[t][:], scalar=coef, in1=y_of[t][:], op0=ALU.add, op1=ALU.mult
+                out=tile_of[t][:], in0=acc_of[t][:], scalar=bias(t), in1=tile_of[t][:], op0=ALU.add, op1=ALU.mult
             )
 
+        def flip_sum(pool, name, first_of, second_of, t):
+            bank = pool.tile([P, N_TILE], F32, name=name)
+            for j in range(4):
+                blk = slice(j * P, (j + 1) * P)
+                nc.tensor.matmul(out=bank[:, blk], lhsT=first_of[t][:, blk], rhs=ident[:], is_transpose=True, start=True, stop=False)
+                nc.tensor.matmul(out=bank[:, blk], lhsT=second_of[t][:, blk], rhs=ident[:], is_transpose=True, start=False, stop=True)
+            return bank
+
         def den_abs(t):
-            nc.scalar.activation(out=den_of[t][:], in_=den_of[t][:], func=ACT.Abs)
+            den = work.tile([P, N_TILE], F32, name="den", bufs=6)
+            nc.scalar.activation(out=den[:], in_=u_of[t][:], func=ACT.Abs)
+            den_of[t] = den
 
         def den_rsqrt(t):
             nc.scalar.activation(out=den_of[t][:], in_=den_of[t][:], func=ACT.Abs_reciprocal_sqrt, bias=ones[:], scale=1.0)
 
         def den_square(t):
-            rec = work.tile([P, N_TILE], F32, name="rec", bufs=2)
-            nc.gpsimd.tensor_tensor(out=rec[:], in0=den_of[t][:], in1=den_of[t][:], op=ALU.mult)
-            rec_of[t] = rec
+            nc.scalar.activation(out=den_of[t][:], in_=den_of[t][:], func=ACT.Square)
 
         def finish(t):
             g, nb, oc = where(t)
             tok = slice(nb * N_TILE, (nb + 1) * N_TILE)
-            nc.vector.scalar_tensor_tensor(
-                out=num_of[t][:], in0=num_of[t][:], scalar=pcoef(t, 0), in1=rec_of[t][:], op0=ALU.add, op1=ALU.mult
-            )
+            nc.vector.tensor_tensor(out=den_of[t][:], in0=n_of[t][:], in1=den_of[t][:], op=ALU.mult)
             nc.sync.dma_start(
                 out=out[tok, g * K_OUT + oc * P : g * K_OUT + (oc + 1) * P].rearrange("(j n) o -> n j o", n=P),
-                in_=num_of[t][:].rearrange("n (j o) -> n j o", j=4),
+                in_=den_of[t][:].rearrange("n (j o) -> n j o", j=4),
             )
 
         def live(t):
@@ -219,6 +231,7 @@ def tile_groupkanlayer_kernel(tc, x_bytes, x_scale, W, b, p, q, out):
 
         for j in range(4):
             x_widen(j)
+            x_turn(j)
             w_interleave(0, j)
             if j % 2 == 1:
                 x_exit(j)
@@ -227,38 +240,42 @@ def tile_groupkanlayer_kernel(tc, x_bytes, x_scale, W, b, p, q, out):
         prepare_parameters()
 
         X_LEAD = 7
-        for s in range(-3, TILES + 4):
+        for s in range(-4, TILES + 5):
             j = s + X_LEAD
-            if live(s):
-                den_first(s)
+            if live(s - 1):
+                u_of[s - 1] = flip_sum(ps_u, "u", c_of, d_of, s - 1)
+            if live(s + 1):
+                mm(s + 1, True)
+            if live(s - 2):
+                den_abs(s - 2)
             if 4 <= j < TILES:
                 x_widen(j)
-            if live(s + 1):
-                add_bias(s + 1)
-                flip(s + 1)
-            if (s + 3) % 4 == 0 and 1 <= (s + 3) // 4 < GROUPS * HALVES:
-                x_quantize((s + 3) // 4)
+            if (s + 2) % 4 == 0 and 1 <= (s + 2) // 4 < GROUPS * HALVES:
+                x_quantize((s + 2) // 4)
             if (s + 4) % 8 == 0 and 1 <= (s + 4) // 8 < GROUPS:
                 w_quantize((s + 4) // 8)
+            if live(s + 1):
+                square_y(s + 1)
+            if live(s):
+                aff_c(s)
+                aff_a(s)
+                aff_b(s)
+            if live(s + 1):
+                aff_d(s + 1)
+            if live(s - 2):
+                den_rsqrt(s - 2)
             if live(s - 4):
                 finish(s - 4)
-            if live(s - 2):
-                den_square(s - 2)
+            if live(s - 3):
+                n_of[s - 3] = flip_sum(ps_n, "n", a_of, s_of, s - 3)
             if live(s):
-                num_first(s)
-            if live(s - 1):
-                times_y(num_of, s - 1)
-                den_abs(s - 1)
-            if live(s):
-                times_y(den_of, s)
-            if live(s + 2):
-                mm(s + 2)
-            if 4 <= j < TILES and j % 2 == 1:
-                x_exit(j)
-            if s % 2 == 1 and 1 <= (s + 11) // 8 < GROUPS:
-                w_interleave((s + 11) // 8, ((s + 11) % 8) // 2)
-            if live(s - 1):
-                plus_times_y(num_of, s - 1, pcoef(s - 1, 1))
-                den_rsqrt(s - 1)
-            if live(s):
-                plus_times_y(den_of, s, qcoef(s, 0))
+                times_y(c_of, s)
+                times_y(a_of, s)
+            if 4 <= j - 1 < TILES and (j - 1) % 2 == 1:
+                x_exit(j - 1)
+            if s % 2 == 0 and 1 <= (s + 12) // 8 < GROUPS:
+                w_interleave((s + 12) // 8, ((s + 12) % 8) // 2)
+            if 4 <= j < TILES:
+                x_turn(j)
+            if live(s - 3):
+                den_square(s - 3)

@@ -31,8 +31,8 @@ def tile_groupkanlayer_kernel(tc, x_bytes, x_scale, W, b, p, q, out):
         xstage = ctx.enter_context(tc.tile_pool(name="xstage", bufs=4))
         gstage = ctx.enter_context(tc.tile_pool(name="gstage", bufs=2))
         work = ctx.enter_context(tc.tile_pool(name="work", bufs=4))
-        ps_x = ctx.enter_context(tc.psum_pool(name="ps_x", bufs=2))
-        ps_a = ctx.enter_context(tc.psum_pool(name="ps_a", bufs=2))
+        ps_x = ctx.enter_context(tc.psum_pool(name="ps_x", bufs=1))
+        ps_a = ctx.enter_context(tc.psum_pool(name="ps_a", bufs=3))
         ps_u = ctx.enter_context(tc.psum_pool(name="ps_u", bufs=2))
         ps_n = ctx.enter_context(tc.psum_pool(name="ps_n", bufs=2))
 
@@ -92,6 +92,7 @@ def tile_groupkanlayer_kernel(tc, x_bytes, x_scale, W, b, p, q, out):
 
         state = {}
         grp_of = {}
+        xs_of = {}
 
         def w_interleave(g, piece):
             if piece == 0:
@@ -111,18 +112,16 @@ def tile_groupkanlayer_kernel(tc, x_bytes, x_scale, W, b, p, q, out):
             rt = nb * 4 + i
             if i == 0:
                 grp_of[c] = gstage.tile([P, 4 * N_TILE], BF16, name="grp", align_bytes=64)
-            if i % 2 == 0:
-                state["xt"] = ps_x.tile([P, 2, 2, P], F32, name="xt")
             xs = xstage.tile([P, K_IN], BF16, name="xs")
             nc.vector.tensor_tensor(out=xs[:], in0=xb[g][:, rt, :].bitcast(FP8), in1=sc[g][:], op=ALU.mult)
-            state["xs"] = xs
+            xs_of[j] = xs
 
-        def x_turn(j):
-            words = state["xs"][:].bitcast(F32)
-            for u in range(2):
-                nc.tensor.transpose(state["xt"][:, j % 2, u, :], words[:, u : K_IN // 2 : 2], ident[:])
-            if j % 2 == 1:
-                state["xt_done"] = state["xt"]
+        def x_turn_pair(j):
+            state["xt"] = ps_x.tile([P, 2, 2, P], F32, name="xt")
+            for a in range(2):
+                words = xs_of[j - 1 + a][:].bitcast(F32)
+                for u in range(2):
+                    nc.tensor.transpose(state["xt"][:, a, u, :], words[:, u : K_IN // 2 : 2], ident[:])
 
         def x_exit(j):
             pair = (j % 4) // 2
@@ -130,7 +129,7 @@ def tile_groupkanlayer_kernel(tc, x_bytes, x_scale, W, b, p, q, out):
                 out=grp_of[j // 4][:].bitcast(F32)[:, pair * 512 : (pair + 1) * 512].rearrange(
                     "p (a r u) -> p a r u", a=2, u=2
                 ),
-                in_=state["xt_done"][:].rearrange("p a u r -> p a r u"),
+                in_=state["xt"][:].rearrange("p a u r -> p a r u"),
             )
 
         def x_quantize(c):
@@ -231,27 +230,29 @@ def tile_groupkanlayer_kernel(tc, x_bytes, x_scale, W, b, p, q, out):
 
         for j in range(4):
             x_widen(j)
-            x_turn(j)
             w_interleave(0, j)
             if j % 2 == 1:
+                x_turn_pair(j)
                 x_exit(j)
         w_quantize(0)
         x_quantize(0)
         prepare_parameters()
 
-        X_LEAD = 7
+        X_LEAD = 8
         for s in range(-4, TILES + 5):
             j = s + X_LEAD
             if live(s - 1):
                 u_of[s - 1] = flip_sum(ps_u, "u", c_of, d_of, s - 1)
-            if live(s + 1):
-                mm(s + 1, True)
+            if s % 2 == 0:
+                for t in (s + 1, s + 2):
+                    if live(t):
+                        mm(t, True)
             if live(s - 2):
                 den_abs(s - 2)
             if 4 <= j < TILES:
                 x_widen(j)
-            if (s + 2) % 4 == 0 and 1 <= (s + 2) // 4 < GROUPS * HALVES:
-                x_quantize((s + 2) // 4)
+            if (s + 3) % 4 == 0 and 1 <= (s + 3) // 4 < GROUPS * HALVES:
+                x_quantize((s + 3) // 4)
             if (s + 4) % 8 == 0 and 1 <= (s + 4) // 8 < GROUPS:
                 w_quantize((s + 4) // 8)
             if live(s + 1):
@@ -273,9 +274,9 @@ def tile_groupkanlayer_kernel(tc, x_bytes, x_scale, W, b, p, q, out):
                 times_y(a_of, s)
             if 4 <= j - 1 < TILES and (j - 1) % 2 == 1:
                 x_exit(j - 1)
-            if s % 2 == 0 and 1 <= (s + 12) // 8 < GROUPS:
-                w_interleave((s + 12) // 8, ((s + 12) % 8) // 2)
-            if 4 <= j < TILES:
-                x_turn(j)
+            if s % 2 == 1 and 1 <= (s + 11) // 8 < GROUPS:
+                w_interleave((s + 11) // 8, ((s + 11) % 8) // 2)
+            if 4 <= j < TILES and j % 2 == 1:
+                x_turn_pair(j)
             if live(s - 3):
                 den_square(s - 3)

@@ -179,9 +179,12 @@ def tile_groupkanlayer_kernel(tc, x_bytes, x_scale, W, b, p, q, out):
             nc.vector.tensor_scalar(out=c[:], in0=s_of[t][:], scalar1=qcoef(t, 2), scalar2=qcoef(t, 0), op0=ALU.mult, op1=ALU.add)
             c_of[t] = c
 
-        def aff_a(t):
-            a = work.tile([P, N_TILE], F32, name="a", bufs=5)
-            nc.vector.tensor_scalar(out=a[:], in0=s_of[t][:], scalar1=pcoef(t, 3), scalar2=pcoef(t, 1), op0=ALU.mult, op1=ALU.add)
+        def aff_a(t, on_scalar):
+            a = work.tile([P, N_TILE], F32, name="a", bufs=6)
+            if on_scalar:
+                nc.scalar.activation(out=a[:], in_=s_of[t][:], func=ACT.Identity, bias=pcoef(t, 1), scale=pcoef(t, 3))
+            else:
+                nc.vector.tensor_scalar(out=a[:], in0=s_of[t][:], scalar1=pcoef(t, 3), scalar2=pcoef(t, 1), op0=ALU.mult, op1=ALU.add)
             a_of[t] = a
 
         def aff_d(t):
@@ -259,7 +262,8 @@ def tile_groupkanlayer_kernel(tc, x_bytes, x_scale, W, b, p, q, out):
                 square_y(s + 1)
             if live(s):
                 aff_c(s)
-                aff_a(s)
+                if s % 2 == 0:
+                    aff_a(s, False)
                 aff_b(s)
             if live(s + 1):
                 aff_d(s + 1)
@@ -280,3 +284,5 @@ def tile_groupkanlayer_kernel(tc, x_bytes, x_scale, W, b, p, q, out):
                 x_turn_pair(j)
             if live(s - 3):
                 den_square(s - 3)
+            if live(s + 1) and (s + 1) % 2 == 1:
+                aff_a(s + 1, True)

@@ -170,17 +170,17 @@ def tile_groupkanlayer_kernel(tc, x_bytes, x_scale, W, b, p, q, out):
             )
 
         def square_y(t):
-            s = work.tile([P, N_TILE], F32, name="s", bufs=7)
+            s = work.tile([P, N_TILE], F32, name="s", bufs=8)
             nc.scalar.activation(out=s[:], in_=acc_of[t][:], func=ACT.Square, bias=bias(t), scale=1.0)
             s_of[t] = s
 
         def aff_c(t):
-            c = work.tile([P, N_TILE], F32, name="c", bufs=3)
+            c = work.tile([P, N_TILE], F32, name="c", bufs=4)
             nc.vector.tensor_scalar(out=c[:], in0=s_of[t][:], scalar1=qcoef(t, 2), scalar2=qcoef(t, 0), op0=ALU.mult, op1=ALU.add)
             c_of[t] = c
 
         def aff_a(t, on_scalar):
-            a = work.tile([P, N_TILE], F32, name="a", bufs=6)
+            a = work.tile([P, N_TILE], F32, name="a", bufs=7)
             if on_scalar:
                 nc.scalar.activation(out=a[:], in_=s_of[t][:], func=ACT.Identity, bias=pcoef(t, 1), scale=pcoef(t, 3))
             else:
@@ -188,7 +188,7 @@ def tile_groupkanlayer_kernel(tc, x_bytes, x_scale, W, b, p, q, out):
             a_of[t] = a
 
         def aff_d(t):
-            d = work.tile([P, N_TILE], F32, name="d", bufs=4)
+            d = work.tile([P, N_TILE], F32, name="d", bufs=5)
             nc.gpsimd.tensor_scalar(out=d[:], in0=s_of[t][:], scalar1=qcoef(t, 1), scalar2=0.0, op0=ALU.mult, op1=ALU.add)
             d_of[t] = d
 
@@ -242,16 +242,16 @@ def tile_groupkanlayer_kernel(tc, x_bytes, x_scale, W, b, p, q, out):
         prepare_parameters()
 
         X_LEAD = 8
-        for s in range(-4, TILES + 5):
+        for s in range(-4, TILES + 6):
             j = s + X_LEAD
-            if live(s - 1):
-                u_of[s - 1] = flip_sum(ps_u, "u", c_of, d_of, s - 1)
+            if live(s - 2):
+                u_of[s - 2] = flip_sum(ps_u, "u", c_of, d_of, s - 2)
             if s % 2 == 0:
                 for t in (s + 1, s + 2):
                     if live(t):
                         mm(t, True)
-            if live(s - 2):
-                den_abs(s - 2)
+            if live(s - 3):
+                den_abs(s - 3)
             if 4 <= j < TILES:
                 x_widen(j)
             if (s + 3) % 4 == 0 and 1 <= (s + 3) // 4 < GROUPS * HALVES:
@@ -267,12 +267,12 @@ def tile_groupkanlayer_kernel(tc, x_bytes, x_scale, W, b, p, q, out):
                 aff_b(s)
             if live(s + 1):
                 aff_d(s + 1)
-            if live(s - 2):
-                den_rsqrt(s - 2)
-            if live(s - 4):
-                finish(s - 4)
             if live(s - 3):
-                n_of[s - 3] = flip_sum(ps_n, "n", a_of, s_of, s - 3)
+                den_rsqrt(s - 3)
+            if live(s - 5):
+                finish(s - 5)
+            if live(s - 4):
+                n_of[s - 4] = flip_sum(ps_n, "n", a_of, s_of, s - 4)
             if live(s):
                 times_y(c_of, s)
                 times_y(a_of, s)
@@ -282,7 +282,7 @@ def tile_groupkanlayer_kernel(tc, x_bytes, x_scale, W, b, p, q, out):
                 w_interleave((s + 11) // 8, ((s + 11) % 8) // 2)
             if 4 <= j < TILES and j % 2 == 1:
                 x_turn_pair(j)
-            if live(s - 3):
-                den_square(s - 3)
-            if live(s + 1) and (s + 1) % 2 == 1:
+            if live(s - 4):
+                den_square(s - 4)
+            if live(s + 1) and not ((s + 1) % 2 == 0):
                 aff_a(s + 1, True)

@@ -262,7 +262,7 @@ def tile_groupkanlayer_kernel(tc, x_bytes, x_scale, W, b, p, q, out):
                 square_y(s + 1)
             if live(s):
                 aff_c(s)
-                if s % 2 == 0:
+                if s % 4 != 1:
                     aff_a(s, False)
                 aff_b(s)
             if live(s + 1):
@@ -284,5 +284,5 @@ def tile_groupkanlayer_kernel(tc, x_bytes, x_scale, W, b, p, q, out):
                 x_turn_pair(j)
             if live(s - 4):
                 den_square(s - 4)
-            if live(s + 1) and not ((s + 1) % 2 == 0):
+            if live(s + 1) and not ((s + 1) % 4 != 1):
                 aff_a(s + 1, True)

@@ -79,7 +79,7 @@ def tile_groupkanlayer_kernel(tc, x_bytes, x_scale, W, b, p, q, out):
 
         def prepare_parameters():
             nc.vector.tensor_copy(out=b_f[:], in_=b_rows[:])
-            b_ps = ps_x.tile([P, P], F32, name="xt")
+            b_ps = ps_n.tile([P, P], F32, name="n")
             nc.tensor.transpose(b_ps[:], b_f[:], ident[:])
             nc.vector.tensor_copy(out=p_f[:], in_=p_bf[:])
             nc.vector.tensor_copy(out=q_f[:], in_=q_bf[:])
@@ -94,11 +94,14 @@ def tile_groupkanlayer_kernel(tc, x_bytes, x_scale, W, b, p, q, out):
         grp_of = {}
         xs_of = {}
 
-        def w_interleave(g, piece):
+        def w_interleave(g, piece, on_vector=False):
             if piece == 0:
                 state["w_grp"] = wstage.tile([P, K_OUT, 4], BF16, name="w_grp", align_bytes=64)
             och = slice(piece * P, (piece + 1) * P)
-            nc.scalar.copy(out=state["w_grp"][:, och, :], in_=w_raw[g][:, :, och].rearrange("p j o -> p o j"))
+            if on_vector:
+                nc.vector.tensor_copy(out=state["w_grp"][:, och, :], in_=w_raw[g][:, :, och].rearrange("p j o -> p o j"))
+            else:
+                nc.scalar.copy(out=state["w_grp"][:, och, :], in_=w_raw[g][:, :, och].rearrange("p j o -> p o j"))
 
         def w_quantize(g):
             nc.vector.quantize_mx(
@@ -233,13 +236,20 @@ def tile_groupkanlayer_kernel(tc, x_bytes, x_scale, W, b, p, q, out):
 
         for j in range(4):
             x_widen(j)
-            w_interleave(0, j)
+            if j < 2:
+                w_interleave(0, j)
             if j % 2 == 1:
                 x_turn_pair(j)
                 x_exit(j)
+        w_interleave(0, 2, True)
+        w_interleave(0, 3, True)
+        prepare_parameters()
         w_quantize(0)
         x_quantize(0)
-        prepare_parameters()
+        for t in range(3):
+            mm(t, True)
+        square_y(0)
+        aff_d(0)
 
         X_LEAD = 8
         for s in range(-4, TILES + 6):
@@ -248,7 +258,7 @@ def tile_groupkanlayer_kernel(tc, x_bytes, x_scale, W, b, p, q, out):
                 u_of[s - 2] = flip_sum(ps_u, "u", c_of, d_of, s - 2)
             if s % 2 == 0:
                 for t in (s + 1, s + 2):
-                    if live(t):
+                    if live(t) and t > 2:
                         mm(t, True)
             if live(s - 3):
                 den_abs(s - 3)
@@ -258,14 +268,14 @@ def tile_groupkanlayer_kernel(tc, x_bytes, x_scale, W, b, p, q, out):
                 x_quantize((s + 3) // 4)
             if (s + 4) % 8 == 0 and 1 <= (s + 4) // 8 < GROUPS:
                 w_quantize((s + 4) // 8)
-            if live(s + 1):
+            if live(s + 1) and s + 1 > 0:
                 square_y(s + 1)
             if live(s):
                 aff_c(s)
                 if s % 4 != 1:
                     aff_a(s, False)
                 aff_b(s)
-            if live(s + 1):
+            if live(s + 1) and s + 1 > 0:
                 aff_d(s + 1)
             if live(s - 3):
                 den_rsqrt(s - 3)

@@ -262,8 +262,6 @@ def tile_groupkanlayer_kernel(tc, x_bytes, x_scale, W, b, p, q, out):
                         mm(t, True)
             if live(s - 3):
                 den_abs(s - 3)
-            if 4 <= j < TILES:
-                x_widen(j)
             if (s + 3) % 4 == 0 and 1 <= (s + 3) // 4 < GROUPS * HALVES:
                 x_quantize((s + 3) // 4)
             if (s + 4) % 8 == 0 and 1 <= (s + 4) // 8 < GROUPS:
@@ -274,6 +272,9 @@ def tile_groupkanlayer_kernel(tc, x_bytes, x_scale, W, b, p, q, out):
                 aff_c(s)
                 if s % 4 != 1:
                     aff_a(s, False)
+            if 4 <= j < TILES:
+                x_widen(j)
+            if live(s):
                 aff_b(s)
             if live(s + 1) and s + 1 > 0:
                 aff_d(s + 1)

@@ -252,7 +252,7 @@ def tile_groupkanlayer_kernel(tc, x_bytes, x_scale, W, b, p, q, out):
         aff_d(0)
 
         X_LEAD = 8
-        for s in range(-4, TILES + 6):
+        for s in range(-5, TILES + 6):
             j = s + X_LEAD
             if live(s - 2):
                 u_of[s - 2] = flip_sum(ps_u, "u", c_of, d_of, s - 2)
@@ -272,8 +272,8 @@ def tile_groupkanlayer_kernel(tc, x_bytes, x_scale, W, b, p, q, out):
                 aff_c(s)
                 if s % 4 != 1:
                     aff_a(s, False)
-            if 4 <= j < TILES:
-                x_widen(j)
+            if 4 <= j + 1 < TILES:
+                x_widen(j + 1)
             if live(s):
                 aff_b(s)
             if live(s + 1) and s + 1 > 0:

@@ -141,6 +141,7 @@ def tile_groupkanlayer_kernel(tc, x_bytes, x_scale, W, b, p, q, out):
             nc.vector.quantize_mx(out=xc[g][:, tok].bitcast(FP8X4), scales=xsc[g][:, tok], in_=grp_of[c][:])
 
         TILES = GROUPS * HALVES * O_TILES
+        DRAIN = 4
         acc_of, s_of, c_of, a_of, d_of, u_of, n_of, den_of = {}, {}, {}, {}, {}, {}, {}, {}
 
         def where(t):
@@ -220,7 +221,10 @@ def tile_groupkanlayer_kernel(tc, x_bytes, x_scale, W, b, p, q, out):
             nc.scalar.activation(out=den_of[t][:], in_=den_of[t][:], func=ACT.Abs_reciprocal_sqrt, bias=ones[:], scale=1.0)
 
         def den_square(t):
-            nc.scalar.activation(out=den_of[t][:], in_=den_of[t][:], func=ACT.Square)
+            if t >= TILES - DRAIN:
+                nc.vector.tensor_tensor(out=den_of[t][:], in0=den_of[t][:], in1=den_of[t][:], op=ALU.mult)
+            else:
+                nc.scalar.activation(out=den_of[t][:], in_=den_of[t][:], func=ACT.Square)
 
         def finish(t):
             g, nb, oc = where(t)
@@ -270,7 +274,7 @@ def tile_groupkanlayer_kernel(tc, x_bytes, x_scale, W, b, p, q, out):
                 square_y(s + 1)
             if live(s):
                 aff_c(s)
-                if s % 4 != 1:
+                if s % 4 != 1 or s >= TILES - 8:
                     aff_a(s, False)
             if 4 <= j + 1 < TILES:
                 x_widen(j + 1)
@@ -295,5 +299,5 @@ def tile_groupkanlayer_kernel(tc, x_bytes, x_scale, W, b, p, q, out):
                 x_turn_pair(j)
             if live(s - 4):
                 den_square(s - 4)
-            if live(s + 1) and not ((s + 1) % 4 != 1):
+            if live(s + 1) and (s + 1) % 4 == 1 and s + 1 < TILES - 8:
                 aff_a(s + 1, True)

@@ -258,12 +258,12 @@ def tile_groupkanlayer_kernel(tc, x_bytes, x_scale, W, b, p, q, out):
         X_LEAD = 8
         for s in range(-5, TILES + 6):
             j = s + X_LEAD
+            if s % 2 == 0 and live(s + 1) and s + 1 > 2:
+                mm(s + 1, True)
             if live(s - 2):
                 u_of[s - 2] = flip_sum(ps_u, "u", c_of, d_of, s - 2)
-            if s % 2 == 0:
-                for t in (s + 1, s + 2):
-                    if live(t) and t > 2:
-                        mm(t, True)
+            if s % 2 == 0 and live(s + 2) and s + 2 > 2:
+                mm(s + 2, True)
             if live(s - 3):
                 den_abs(s - 3)
             if (s + 3) % 4 == 0 and 1 <= (s + 3) // 4 < GROUPS * HALVES:

from contextlib import ExitStack

import concourse.mybir as mybir
from concourse.masks import make_identity

ROWS, GROUPS, K_IN, K_OUT = 1024, 8, 512, 512
FLOPS = 2 * ROWS * GROUPS * K_IN * K_OUT

F32 = mybir.dt.float32
BF16 = mybir.dt.bfloat16
U32 = mybir.dt.uint32
U8 = mybir.dt.uint8
FP8 = mybir.dt.float8_e4m3fn
FP8X4 = mybir.dt.float8_e4m3fn_x4
ACT = mybir.ActivationFunctionType
ALU = mybir.AluOpType

P = 128
ROW_TILES = ROWS // P
N_TILE = 512
HALVES = ROWS // N_TILE
O_TILES = K_OUT // P


def tile_groupkanlayer_kernel(tc, x_bytes, x_scale, W, b, p, q, out):
    nc = tc.nc
    with ExitStack() as ctx:
        ctx.enter_context(tc.manual_schedule())
        const = ctx.enter_context(tc.tile_pool(name="const", bufs=1))
        wstage = ctx.enter_context(tc.tile_pool(name="wstage", bufs=2))
        xstage = ctx.enter_context(tc.tile_pool(name="xstage", bufs=4))
        gstage = ctx.enter_context(tc.tile_pool(name="gstage", bufs=2))
        work = ctx.enter_context(tc.tile_pool(name="work", bufs=4))
        ps_x = ctx.enter_context(tc.psum_pool(name="ps_x", bufs=1))
        ps_a = ctx.enter_context(tc.psum_pool(name="ps_a", bufs=3))
        ps_u = ctx.enter_context(tc.psum_pool(name="ps_u", bufs=2))
        ps_n = ctx.enter_context(tc.psum_pool(name="ps_n", bufs=2))

        ones = const.tile([P, 1], F32, name="ones")
        nc.vector.memset(ones[:], 1.0)
        junk = const.tile([P, 1], F32, name="junk")
        nc.scalar.activation(out=junk[:], in_=ones[:], func=ACT.Abs_reciprocal_sqrt)

        ident = const.tile([P, P], F32, name="ident")
        make_identity(nc, ident[:])

        p_bf = const.tile([P, GROUPS * 4], BF16, name="p_bf")
        q_bf = const.tile([P, GROUPS * 3], BF16, name="q_bf")
        b_rows = const.tile([P, P], BF16, name="b_rows")
        nc.vector.memset(b_rows[:].bitcast(F32), 0.0)

        xb, sc, w_raw = [], [], []
        scale_row = x_scale.rearrange("o k -> (o k)")
        for g in range(GROUPS):
            cols = slice(g * K_IN, (g + 1) * K_IN)
            sc_g = const.tile([P, K_IN], F32, name="sc%d" % g)
            nc.sync.dma_start(out=sc_g[:], in_=scale_row[cols].partition_broadcast(P))
            xb_g = const.tile([P, ROW_TILES, K_IN], U8, name="xbytes%d" % g)
            x_view = x_bytes[:, cols].rearrange("(r p) c -> p r c", p=P)
            if g == 0:
                nc.sync.dma_start(out=xb_g[:, 0:4, :], in_=x_view[:, 0:4, :])
            w_g = const.tile([P, 4, K_OUT], BF16, name="wraw%d" % g)
            nc.sync.dma_start(out=w_g[:], in_=W[g].rearrange("(p j) o -> p j o", j=4))
            if g == 0:
                nc.sync.dma_start(out=xb_g[:, 4:8, :], in_=x_view[:, 4:8, :])
                nc.sync.dma_start(out=b_rows[0 : GROUPS * O_TILES, :], in_=b.rearrange("g (c o) -> (g c) o", o=P))
                nc.sync.dma_start(out=p_bf[:], in_=p.rearrange("g c -> (g c)").partition_broadcast(P))
                nc.sync.dma_start(out=q_bf[:], in_=q.rearrange("g c -> (g c)").partition_broadcast(P))
            else:
                nc.sync.dma_start(out=xb_g[:], in_=x_view)
            sc.append(sc_g)
            xb.append(xb_g)
            w_raw.append(w_g)

        p_f = const.tile([P, GROUPS * 4], F32, name="p_f")
        q_f = const.tile([P, GROUPS * 3], F32, name="q_f")
        b_f = const.tile([P, P], F32, name="b_f")
        bT = const.tile([P, GROUPS * O_TILES], F32, name="bT")

        def prepare_parameters():
            nc.vector.tensor_copy(out=b_f[:], in_=b_rows[:])
            b_ps = ps_n.tile([P, P], F32, name="n")
            nc.tensor.transpose(b_ps[:], b_f[:], ident[:])
            nc.vector.tensor_copy(out=p_f[:], in_=p_bf[:])
            nc.vector.tensor_copy(out=q_f[:], in_=q_bf[:])
            nc.vector.tensor_copy(out=bT[:], in_=b_ps[:, 0 : GROUPS * O_TILES])

        xc = [const.tile([P, ROWS], U32, name="xc%d" % g, align_bytes=64) for g in range(GROUPS)]
        xsc = [const.tile([P, ROWS], U8, name="xsc%d" % g, align_bytes=64) for g in range(GROUPS)]
        wc = [const.tile([P, K_OUT], U32, name="wc%d" % g, align_bytes=64) for g in range(GROUPS)]
        wsc = [const.tile([P, K_OUT], U8, name="wsc%d" % g, align_bytes=64) for g in range(GROUPS)]

        state = {}
        grp_of = {}
        xs_of = {}

        def w_interleave(g, piece, on_vector=False):
            if piece == 0:
                state["w_grp"] = wstage.tile([P, K_OUT, 4], BF16, name="w_grp", align_bytes=64)
            och = slice(piece * P, (piece + 1) * P)
            if on_vector:
                nc.vector.tensor_copy(out=state["w_grp"][:, och, :], in_=w_raw[g][:, :, och].rearrange("p j o -> p o j"))
            else:
                nc.scalar.copy(out=state["w_grp"][:, och, :], in_=w_raw[g][:, :, och].rearrange("p j o -> p o j"))

        def w_quantize(g):
            nc.vector.quantize_mx(
                out=wc[g][:].bitcast(FP8X4), scales=wsc[g][:],
                in_=state["w_grp"][:].rearrange("p o j -> p (o j)"),
            )

        def x_widen(j):
            c, i = divmod(j, 4)
            g, nb = divmod(c, HALVES)
            rt = nb * 4 + i
            if i == 0:
                grp_of[c] = gstage.tile([P, 4 * N_TILE], BF16, name="grp", align_bytes=64)
            xs = xstage.tile([P, K_IN], BF16, name="xs")
            nc.vector.tensor_tensor(out=xs[:], in0=xb[g][:, rt, :].bitcast(FP8), in1=sc[g][:], op=ALU.mult)
            xs_of[j] = xs

        def x_turn_pair(j):
            state["xt"] = ps_x.tile([P, 2, 2, P], F32, name="xt")
            for a in range(2):
                words = xs_of[j - 1 + a][:].bitcast(F32)
                for u in range(2):
                    nc.tensor.transpose(state["xt"][:, a, u, :], words[:, u : K_IN // 2 : 2], ident[:])

        def x_exit(j):
            pair = (j % 4) // 2
            nc.scalar.copy(
                out=grp_of[j // 4][:].bitcast(F32)[:, pair * 512 : (pair + 1) * 512].rearrange(
                    "p (a r u) -> p a r u", a=2, u=2
                ),
                in_=state["xt"][:].rearrange("p a u r -> p a r u"),
            )

        def x_quantize(c):
            g, nb = divmod(c, HALVES)
            tok = slice(nb * N_TILE, (nb + 1) * N_TILE)
            nc.vector.quantize_mx(out=xc[g][:, tok].bitcast(FP8X4), scales=xsc[g][:, tok], in_=grp_of[c][:])

        TILES = GROUPS * HALVES * O_TILES
        DRAIN = 4
        acc_of, s_of, c_of, a_of, d_of, u_of, n_of, den_of = {}, {}, {}, {}, {}, {}, {}, {}

        def where(t):
            c, oc = divmod(t, O_TILES)
            g, nb = divmod(c, HALVES)
            return g, nb, oc

        def pcoef(t, i):
            g = where(t)[0]
            return p_f[:, 4 * g + i : 4 * g + i + 1]

        def qcoef(t, i):
            g = where(t)[0]
            return q_f[:, 3 * g + i : 3 * g + i + 1]

        def bias(t):
            g, nb, oc = where(t)
            col = g * O_TILES + oc
            return bT[:, col : col + 1]

        def mm(t, first):
            g, nb, oc = where(t)
            tok = slice(nb * N_TILE, (nb + 1) * N_TILE)
            och = slice(oc * P, (oc + 1) * P)
            if first:
                acc_of[t] = ps_a.tile([P, N_TILE], F32, name="acc")
            nc.tensor.matmul_mx(
                out=acc_of[t][:], lhsT=wc[g][:, och].bitcast(FP8X4), lhsT_scale=wsc[g][:, och],
                rhs=xc[g][:, tok].bitcast(FP8X4), rhs_scale=xsc[g][:, tok], start=True, stop=True,
            )

        def square_y(t):
            s = work.tile([P, N_TILE], F32, name="s", bufs=8)
            nc.scalar.activation(out=s[:], in_=acc_of[t][:], func=ACT.Square, bias=bias(t), scale=1.0)
            s_of[t] = s

        def aff_c(t):
            c = work.tile([P, N_TILE], F32, name="c", bufs=4)
            nc.vector.tensor_scalar(out=c[:], in0=s_of[t][:], scalar1=qcoef(t, 2), scalar2=qcoef(t, 0), op0=ALU.mult, op1=ALU.add)
            c_of[t] = c

        def aff_a(t, on_scalar):
            a = work.tile([P, N_TILE], F32, name="a", bufs=7)
            if on_scalar:
                nc.scalar.activation(out=a[:], in_=s_of[t][:], func=ACT.Identity, bias=pcoef(t, 1), scale=pcoef(t, 3))
            else:
                nc.vector.tensor_scalar(out=a[:], in0=s_of[t][:], scalar1=pcoef(t, 3), scalar2=pcoef(t, 1), op0=ALU.mult, op1=ALU.add)
            a_of[t] = a

        def aff_d(t):
            d = work.tile([P, N_TILE], F32, name="d", bufs=5)
            nc.gpsimd.tensor_scalar(out=d[:], in0=s_of[t][:], scalar1=qcoef(t, 1), scalar2=0.0, op0=ALU.mult, op1=ALU.add)
            d_of[t] = d

        def aff_b(t):
            nc.gpsimd.tensor_scalar(out=s_of[t][:], in0=s_of[t][:], scalar1=pcoef(t, 2), scalar2=pcoef(t, 0), op0=ALU.mult, op1=ALU.add)

        def times_y(tile_of, t):
            nc.vector.scalar_tensor_tensor(
                out=tile_of[t][:], in0=acc_of[t][:], scalar=bias(t), in1=tile_of[t][:], op0=ALU.add, op1=ALU.mult
            )

        def flip_sum(pool, name, first_of, second_of, t):
            bank = pool.tile([P, N_TILE], F32, name=name)
            for j in range(4):
                blk = slice(j * P, (j + 1) * P)
                nc.tensor.matmul(out=bank[:, blk], lhsT=first_of[t][:, blk], rhs=ident[:], is_transpose=True, start=True, stop=False)
                nc.tensor.matmul(out=bank[:, blk], lhsT=second_of[t][:, blk], rhs=ident[:], is_transpose=True, start=False, stop=True)
            return bank

        def den_abs(t):
            den = work.tile([P, N_TILE], F32, name="den", bufs=6)
            nc.scalar.activation(out=den[:], in_=u_of[t][:], func=ACT.Abs)
            den_of[t] = den

        def den_rsqrt(t):
            nc.scalar.activation(out=den_of[t][:], in_=den_of[t][:], func=ACT.Abs_reciprocal_sqrt, bias=ones[:], scale=1.0)

        def den_square(t):
            if t >= TILES - DRAIN:
                nc.vector.tensor_tensor(out=den_of[t][:], in0=den_of[t][:], in1=den_of[t][:], op=ALU.mult)
            else:
                nc.scalar.activation(out=den_of[t][:], in_=den_of[t][:], func=ACT.Square)

        def finish(t):
            g, nb, oc = where(t)
            tok = slice(nb * N_TILE, (nb + 1) * N_TILE)
            nc.vector.tensor_tensor(out=den_of[t][:], in0=n_of[t][:], in1=den_of[t][:], op=ALU.mult)
            nc.sync.dma_start(
                out=out[tok, g * K_OUT + oc * P : g * K_OUT + (oc + 1) * P].rearrange("(j n) o -> n j o", n=P),
                in_=den_of[t][:].rearrange("n (j o) -> n j o", j=4),
            )

        def live(t):
            return 0 <= t < TILES

        for j in range(4):
            x_widen(j)
            if j < 2:
                w_interleave(0, j)
            if j % 2 == 1:
                x_turn_pair(j)
                x_exit(j)
        w_interleave(0, 2, True)
        w_interleave(0, 3, True)
        prepare_parameters()
        w_quantize(0)
        x_quantize(0)
        for t in range(3):
            mm(t, True)
        square_y(0)
        aff_d(0)

        X_LEAD = 8
        for s in range(-5, TILES + 6):
            j = s + X_LEAD
            if s % 2 == 0 and live(s + 1) and s + 1 > 2:
                mm(s + 1, True)
            if live(s - 2):
                u_of[s - 2] = flip_sum(ps_u, "u", c_of, d_of, s - 2)
            if s % 2 == 0 and live(s + 2) and s + 2 > 2:
                mm(s + 2, True)
            if live(s - 3):
                den_abs(s - 3)
            if (s + 3) % 4 == 0 and 1 <= (s + 3) // 4 < GROUPS * HALVES:
                x_quantize((s + 3) // 4)
            if (s + 4) % 8 == 0 and 1 <= (s + 4) // 8 < GROUPS:
                w_quantize((s + 4) // 8)
            if live(s + 1) and s + 1 > 0:
                square_y(s + 1)
            if live(s):
                aff_c(s)
                if s % 4 != 1 or s >= TILES - 8:
                    aff_a(s, False)
            if 4 <= j + 1 < TILES:
                x_widen(j + 1)
            if live(s):
                aff_b(s)
            if live(s + 1) and s + 1 > 0:
                aff_d(s + 1)
            if live(s - 3):
                den_rsqrt(s - 3)
            if live(s - 5):
                finish(s - 5)
            if live(s - 4):
                n_of[s - 4] = flip_sum(ps_n, "n", a_of, s_of, s - 4)
            if live(s):
                times_y(c_of, s)
                times_y(a_of, s)
            if 4 <= j - 1 < TILES and (j - 1) % 2 == 1:
                x_exit(j - 1)
            if s % 2 == 1 and 1 <= (s + 11) // 8 < GROUPS:
                w_interleave((s + 11) // 8, ((s + 11) % 8) // 2)
            if 4 <= j < TILES and j % 2 == 1:
                x_turn_pair(j)
            if live(s - 4):
                den_square(s - 4)
            if live(s + 1) and (s + 1) % 4 == 1 and s + 1 < TILES - 8:
                aff_a(s + 1, True)
